import numpy as np
import ml_dtypes


def mxq(x, axis, fmt="e4m3"):
    dtype, down = {"e4m3": (ml_dtypes.float8_e4m3fn, 7), "e5m2": (ml_dtypes.float8_e5m2, 14)}[fmt]
    v = np.moveaxis(np.asarray(x, np.float32).astype(ml_dtypes.bfloat16).astype(np.float64), axis, -1)
    blocks = v.reshape(v.shape[:-1] + (-1, 32))
    amax = np.abs(blocks).max(-1, keepdims=True)
    byte = np.maximum(np.where(amax > 0, np.frexp(amax)[1] - 1 + 127, 0) - down, 1)
    scale = np.exp2(byte - 127.0)
    codes = (blocks / scale).astype(np.float32).astype(dtype).astype(np.float64)
    return np.moveaxis((codes * scale).reshape(v.shape), -1, axis)


WIDE = False


def mx_kscale(k):
    if not WIDE:
        return np.ones(k)
    levels = np.array([10, -10, 5, -5, 0])
    if k % 512:
        return np.exp2(np.random.permutation(np.resize(levels, k // 32))).repeat(32)
    a = np.empty((k // 512, 16))
    for p in range(k // 512):
        a[p, :8] = np.random.permutation(np.resize(levels, 8))
        for g in range(8):
            far = levels[np.abs(levels - a[p, g]) >= 10]
            a[p, g + 8] = far[np.random.randint(len(far))]
    return np.exp2(a.ravel()).repeat(32)


BF16 = ml_dtypes.bfloat16


def bf(x):
    return np.asarray(x, np.float32).astype(BF16)


def f64(x):
    return np.asarray(x).astype(np.float64)


E2M1 = np.array([0.0, 0.5, 1.0, 1.5, 2.0, 3.0, 4.0, 6.0, -0.0, -0.5, -1.0, -1.5, -2.0, -3.0, -4.0, -6.0])


def pack_weight(w, fmt):
    k, n = w.shape
    w = f64(bf(w)).reshape(k // 32, 32, n)
    amax = np.abs(w).max(1)
    if fmt == "e4m3":
        byte = np.frexp(amax)[1] - 1 + 127 - 7
    else:
        mant, ex = np.frexp(amax / 6.0)
        byte = np.where(mant > 0.5, ex, ex - 1) + 127
    byte = np.clip(np.where(amax > 0, byte, 1), 1, 254)
    scaled = (w * np.exp2(127.0 - byte)[:, None, :]).reshape(k, n).astype(np.float32)
    by_word = np.ascontiguousarray(scaled.reshape(k // 512, 128, 4, n).transpose(0, 1, 3, 2))
    if fmt == "e4m3":
        words = by_word.astype(ml_dtypes.float8_e4m3fn).view(np.uint8)
    else:
        c = by_word.astype(ml_dtypes.float4_e2m1fn).view(np.uint8) & 0xF
        words = c[..., 0::2] | (c[..., 1::2] << 4)
    return np.ascontiguousarray(words), np.ascontiguousarray(byte.astype(np.uint8).reshape(k // 512, 16, n))


def unpack_weight(words, scales, fmt):
    g, p, n, _ = words.shape
    if fmt == "e4m3":
        vals = np.ascontiguousarray(words).view(ml_dtypes.float8_e4m3fn).astype(np.float64)
    else:
        nib = np.empty((g, p, n, 4), np.uint8)
        nib[..., 0::2] = words & 0xF
        nib[..., 1::2] = words >> 4
        vals = E2M1[nib]
    vals = vals * np.repeat(np.exp2(scales.astype(np.float64) - 127.0), 8, axis=1)[..., None]
    return vals.transpose(0, 1, 3, 2).reshape(g * 512, n)
def pack4(w):
    words, scales = pack_weight(w, "e2m1")
    return words.reshape(words.shape[0], 128, -1), scales


def unpack4(words, scales):
    return unpack_weight(words.reshape(words.shape[0], 128, -1, 2), scales, "e2m1")


NB, DI, DO, B = 8, 1024, 1024, 256
F = NB * DO
EPS = 1e-5


def draw0():
    s, t = mx_kscale(DI), mx_kscale(F)
    tk = t.reshape(NB, DO)
    x = bf(np.random.standard_normal((B, DI)) * s)
    W = bf(np.random.standard_normal((NB, DI, DO)) / np.sqrt(DI) / s[None, :, None])
    b = bf(np.random.standard_normal((NB, DO)) * 0.5)
    gamma = bf((1.0 + 0.2 * np.random.standard_normal((NB, DO))) * tk)
    beta = bf(0.2 * np.random.standard_normal((NB, DO)) * tk)
    words, scales = pack4(np.random.standard_normal((F, DO)) / np.sqrt(F) / t[:, None])
    return {"x": x,
            "W": W,
            "b": b,
            "gamma": gamma,
            "beta": beta,
            "Wf1_words": words,
            "Wf1_scales": scales,
            "bf1": bf(np.random.standard_normal(DO) * 0.3)}


def core(x, W, b, gamma, beta, Wf1_words, Wf1_scales, bf1):
    w2 = f64(W).transpose(1, 0, 2).reshape(DI, F)
    h = (mxq(f64(x), 1, "e4m3") @ mxq(w2, 0, "e4m3")).reshape(B, NB, DO) + f64(b)[None]
    h = np.maximum(h, 0.0)
    mean = h.mean(axis=0, keepdims=True)
    var = ((h - mean) ** 2).mean(axis=0, keepdims=True)
    h = (h - mean) * (1.0 / np.sqrt(var + EPS)) * f64(gamma)[None] + f64(beta)[None]
    fused = h.reshape(B, F)
    return np.maximum((mxq(fused, 1, "e4m3") @ unpack4(Wf1_words, Wf1_scales)) + f64(bf1), 0.0)


def e4m3fn_bytes(y):
    return np.clip(np.asarray(y, np.float64), -448.0, 448.0).astype(np.float32).astype(ml_dtypes.float8_e4m3fn).view(np.uint8)


def e4m3fn_values(b):
    return np.asarray(b, np.uint8).view(ml_dtypes.float8_e4m3fn).astype(np.float64)


def setup_inputs():
    d = draw0()
    x0 = np.asarray(d['W']).astype(np.float64)
    s = (np.max(np.abs(x0), axis=(0, 2), keepdims=True) / 448.0).astype(np.float32)
    out = {}
    for k, v in d.items():
        if k == 'W':
            out['W_bytes'] = e4m3fn_bytes(x0 / s.astype(np.float64))
            out['W_scale'] = s
        else:
            out[k] = v
    return out


def reference(x, W_bytes, W_scale, b, gamma, beta, Wf1_words, Wf1_scales, bf1):
    return core(x, e4m3fn_values(W_bytes) * W_scale.astype(np.float64), b, gamma, beta, Wf1_words, Wf1_scales, bf1)

from contextlib import ExitStack

import concourse.mybir as mybir
from concourse.masks import make_identity

F32 = mybir.dt.float32
BF16 = mybir.dt.bfloat16
I32 = mybir.dt.int32
U32 = mybir.dt.uint32
U8 = mybir.dt.uint8
FP8 = mybir.dt.float8_e4m3fn
FP8X4 = mybir.dt.float8_e4m3fn_x4
FP4X4 = mybir.dt.float4_e2m1fn_x4
ACT = mybir.ActivationFunctionType
ALU = mybir.AluOpType

NB, DI, DO, B = 8, 1024, 1024, 256
P = 128
T = 4
KP = P * T
NG = DI // KP
UNITS = NB * DO // KP
EPS = 1e-5

FLOPS = 2 * B * DI * NB * DO + 2 * B * NB * DO * DO


def tile_extremeoptimizationlayer_pa_w4_kernel(tc, x, W_bytes, W_scale, b, gamma, beta, Wf1_words, Wf1_scales, bf1, out):
    nc = tc.nc
    with ExitStack() as ctx:
        keep = ctx.enter_context(tc.tile_pool(name="keep", bufs=1))
        wpool = ctx.enter_context(tc.tile_pool(name="wpool", bufs=4))
        work = ctx.enter_context(tc.tile_pool(name="work", bufs=3))
        hps = ctx.enter_context(tc.psum_pool(name="hps", bufs=4))
        accps = ctx.enter_context(tc.psum_pool(name="accps", bufs=1))
        ctx.enter_context(tc.manual_schedule())

        warm = keep.tile([P, 1], F32, name="warm")
        nc.vector.memset(warm[:], 1.0)
        nc.scalar.activation(warm[:], warm[:], ACT.Sqrt)
        eps = keep.tile([P, 1], F32, name="eps")
        ident = keep.tile([P, P], F32, name="ident")
        make_identity(nc, ident[:])
        vrows = keep.tile([P, KP], BF16, name="vrows")
        nc.vector.memset(vrows[:], 0.0)
        nc.vector.memset(eps[:], 1.0)
        nc.vector.tensor_scalar(eps[:], eps[:], EPS, None, op0=ALU.mult)

        kscale = keep.tile([P, NG * T], F32, name="kscale")
        nc.scalar.dma_start(out=kscale[:].rearrange("p (g t) -> p g t", g=NG), in_=W_scale.rearrange("o (g p t) z -> p (o g) (t z)", p=P, t=T))
        for v, vec_in in enumerate((b, gamma, beta)):
            nc.scalar.dma_start(out=vrows[16 * v : 16 * v + 16, :], in_=vec_in.rearrange("k (h c) -> (k h) c", c=KP))
        x_sb = keep.tile([P, 2, DI], BF16, name="x_sb")

        wbytes = {}

        def load_first_branch():
            src = W_bytes[0].rearrange("(g p t) o -> p g t o", p=P, t=T)
            for half in range(2):
                wb = keep.tile([P, NG, T, KP], U8, name="wb0%d" % half)
                for g in range(NG):
                    nc.sync.dma_start(out=wb[:, g], in_=src[:, g, :, half * KP : (half + 1) * KP])
                    if half == 0 and g == 0:
                        nc.sync.dma_start(out=x_sb[:], in_=x.rearrange("(r p) k -> p r k", p=P))
                wbytes[half] = wb

        def load_branch(k):
            wb = wpool.tile([P, NG, T, DO], U8, name="wb")
            src = W_bytes[k].rearrange("(g p t) o -> p g t o", p=P, t=T)
            for g in range(NG):
                nc.sync.dma_start(out=wb[:, g], in_=src[:, g])
            for half in range(2):
                wbytes[2 * k + half] = wb[:, :, :, half * KP : (half + 1) * KP]

        load_first_branch()
        load_branch(1)

        wf = keep.tile([P, UNITS, 2 * DO], U8, name="wf", align_bytes=64)
        wfs = keep.tile([P, UNITS, DO], U8, name="wfs", align_bytes=64)
        nc.gpsimd.memset(wfs[:].rearrange("p u n -> p (u n)").bitcast(I32), 0)
        for q in range(4):
            nc.sync.dma_start(
                out=wfs[32 * q : 32 * q + 4].bitcast(I32),
                in_=Wf1_scales[:, 4 * q : 4 * q + 4, :].rearrange("u q n -> q u n").bitcast(I32),
            )
        nc.sync.dma_start(out=wf[:, 0:4], in_=Wf1_words[0:4].rearrange("u p n -> p u n"))
        load_branch(2)
        load_branch(3)
        bf1_b = keep.tile([P, DO], BF16, name="bf1_b")

        x_codes = keep.tile([P, NG, B], U32, name="x_codes", align_bytes=64)
        x_scales = keep.tile([P, NG, B], U8, name="x_scales", align_bytes=64)
        x_words = x_sb[:].bitcast(F32)
        x_grouped = []
        for g in range(NG):
            xt = hps.tile([P, 2, 2, P], F32, name="h")
            for r in range(2):
                for u in range(2):
                    nc.tensor.transpose(xt[:, r, u, :], x_words[:, r, 256 * g + u : 256 * (g + 1) : 2], ident[:])
            xg = keep.tile([P, B, T], BF16, name="xg%d" % g, align_bytes=64)
            dst = xg[:].bitcast(F32).rearrange("p (r n) u -> p r n u", r=2)
            src = xt[:].rearrange("p r u n -> p r n u")
            if g == 0:
                nc.scalar.copy(dst, src)
            else:
                nc.scalar.copy(dst, src)
            x_grouped.append(xg)
        vt = hps.tile([P, 2, 2, P], F32, name="h")
        for u in range(2):
            nc.tensor.transpose(vt[:, 0, u, :], vrows[:].bitcast(F32)[:, u::2], ident[:])
        vec16 = keep.tile([P, 48, T], BF16, name="vec16")
        nc.scalar.copy(vec16[:].bitcast(F32), vt[:, 0, :, 0:48].rearrange("p u r -> p r u"))
        vec = keep.tile([P, 48, T], F32, name="vec")
        nc.scalar.copy(vec[:], vec16[:])

        act_codes = keep.tile([P, UNITS, B], U32, name="act_codes", align_bytes=64)
        act_scales = keep.tile([P, UNITS, B], U8, name="act_scales", align_bytes=64)
        acc = {}
        for m in range(2):
            for n in range(2):
                acc[m, n] = accps.tile([P, KP], F32, name="acc%d%d" % (m, n))

        plane, grouped, codes, scales = {}, {}, {}, {}
        h, a, stat, sq, shift, nplane, ngrp = {}, {}, {}, {}, {}, {}, {}

        def widen(i, g):
            wb = wbytes[i]
            plane[i, g] = work.tile([P, 2, KP, 2], BF16, name="plane", align_bytes=64)
            for t in range(T):
                nc.vector.tensor_scalar(
                    plane[i, g][:, t // 2, :, t % 2], wb[:, g, t, :].bitcast(FP8), kscale[:, g * T + t : g * T + t + 1], None, op0=ALU.mult
                )

        def merge(i, g):
            grouped[i, g] = work.tile([P, KP, T], BF16, name="grouped", align_bytes=64)
            dst = grouped[i, g][:].rearrange("p c j -> p (c j)").bitcast(F32).rearrange("p (t m u) -> p m t u", t=T, u=2)
            src = plane[i, g][:].rearrange("p u c e -> p (u c e)").bitcast(F32).rearrange("p (u m t) -> p m t u", u=2, t=T)
            nc.scalar.copy(dst, src)

        def quant(i, g):
            if g == 0:
                codes[i] = work.tile([P, NG, KP], U32, name="codes", align_bytes=64)
                scales[i] = work.tile([P, NG, KP], U8, name="scales", align_bytes=64)
            nc.vector.quantize_mx(codes[i][:, g, :].bitcast(FP8X4), scales[i][:, g, :], grouped[i, g][:].rearrange("p c j -> p (c j)"))

        def mm1(i):
            for half in range(2):
                h[i, half] = hps.tile([P, 2, B], F32, name="h")
                for s in range(2):
                    c = slice(P * (2 * half + s), P * (2 * half + s + 1))
                    for g in range(NG):
                        nc.tensor.matmul_mx(
                            h[i, half][:, s, :],
                            lhsT=codes[i][:, g, c].bitcast(FP8X4),
                            lhsT_scale=scales[i][:, g, c],
                            rhs=x_codes[:, g, :].bitcast(FP8X4),
                            rhs_scale=x_scales[:, g, :],
                            start=(g == 0),
                            stop=(g == NG - 1),
                        )

        def relu(i, half):
            if half == 0:
                a[i] = work.tile([P, T, B], F32, name="a")
                stat[i] = work.tile([P, T], F32, name="stat")
            for s in range(2):
                t = 2 * half + s
                nc.scalar.activation(a[i][:, t, :], h[i, half][:, s, :], ACT.Relu, bias=vec[:, i, t : t + 1], accum_out=stat[i][:, t : t + 1])

        def center(i):
            shift[i] = work.tile([P, T], F32, name="shift")
            nc.vector.tensor_scalar(shift[i][:], stat[i][:], -1.0 / B, None, op0=ALU.mult)
            sq[i] = work.tile([P, T], F32, name="sq")

        def square(i, half):
            for t in (2 * half, 2 * half + 1):
                junk = work.tile([P, B], BF16, name="junk")
                nc.scalar.activation(junk[:], a[i][:, t, :], ACT.Square, bias=shift[i][:, t : t + 1], accum_out=sq[i][:, t : t + 1])

        scl, off = {}, {}

        def root(i):
            std = work.tile([P, T], F32, name="std")
            nc.scalar.activation(std[:], sq[i][:], ACT.Sqrt, bias=eps[:], scale=1.0 / B)
            sq[i] = std

        def coeff(i):
            rs = work.tile([P, T], F32, name="rs")
            nc.vector.reciprocal(rs[:], sq[i][:])
            scl[i] = work.tile([P, T], F32, name="scl")
            off[i] = work.tile([P, T], F32, name="off")
            tmp = work.tile([P, T], F32, name="tmp")
            nc.vector.tensor_tensor(scl[i][:], rs[:], vec[:, 16 + i, :], op=ALU.mult)
            nc.vector.tensor_tensor(tmp[:], shift[i][:], scl[i][:], op=ALU.mult)
            nc.vector.tensor_tensor(off[i][:], tmp[:], vec[:, 32 + i, :], op=ALU.add)

        def norm(i):
            nplane[i] = work.tile([P, 2, B, 2], BF16, name="nplane", align_bytes=64)
            for t in range(T):
                nc.vector.tensor_scalar(
                    nplane[i][:, t // 2, :, t % 2], a[i][:, t, :], scl[i][:, t : t + 1], off[i][:, t : t + 1], op0=ALU.mult, op1=ALU.add
                )

        def nmerge(i):
            ngrp[i] = work.tile([P, B, T], BF16, name="ngrp", align_bytes=64)
            nc.scalar.copy(
                ngrp[i][:].rearrange("p n t -> p (n t)").bitcast(F32).rearrange("p (n u) -> p n u", u=2),
                nplane[i][:].rearrange("p u n e -> p (u n e)").bitcast(F32).rearrange("p (u n) -> p n u", u=2),
            )

        def nquant(i):
            nc.vector.quantize_mx(act_codes[:, i, :].bitcast(FP8X4), act_scales[:, i, :], ngrp[i][:].rearrange("p n t -> p (n t)"))

        def mm2(i):
            for m in range(2):
                rows = slice(P * m, P * (m + 1))
                for n in range(2):
                    nc.tensor.matmul_mx(
                        acc[m, n][:],
                        lhsT=act_codes[:, i, rows].bitcast(FP8X4),
                        lhsT_scale=act_scales[:, i, rows],
                        rhs=wf[:, i, DO * n : DO * (n + 1)].bitcast(FP4X4),
                        rhs_scale=wfs[:, i, KP * n : KP * (n + 1)],
                        start=(i == 0),
                        stop=(i == UNITS - 1),
                    )

        def when(f, i, *args):
            if 0 <= i < UNITS:
                f(i, *args)

        for s in range(UNITS + 3):
            if s % 2 == 0 and 4 <= s // 2 + 3 < NB:
                load_branch(s // 2 + 3)
                if s // 2 <= 3:
                    u = slice(4 * (s // 2), 4 * (s // 2) + 4)
                    nc.sync.dma_start(out=wf[:, u], in_=Wf1_words[u].rearrange("u p n -> p u n"))
            if s == 4:
                nc.sync.dma_start(out=bf1_b[:], in_=bf1.partition_broadcast(P))
            when(widen, s, 0)
            if s == 0:
                for g in range(NG):
                    nc.vector.quantize_mx(x_codes[:, g, :].bitcast(FP8X4), x_scales[:, g, :], x_grouped[g][:].rearrange("p n t -> p (n t)"))
            when(nmerge, s - 3)
            when(square, s - 2, 0)
            when(square, s - 2, 1)
            when(root, s - 2)
            when(merge, s, 0)
            when(quant, s - 1, 1)
            when(mm1, s - 1)
            when(nquant, s - 3)
            when(widen, s, 1)
            when(relu, s - 1, 0)
            when(relu, s - 1, 1)
            when(quant, s, 0)
            when(coeff, s - 2)
            when(norm, s - 2)
            when(center, s - 1)
            when(merge, s, 1)
            when(mm2, s - 3)

        for m in range(2):
            for n in range(2):
                z = work.tile([P, KP], F32, name="z")
                cols = slice(KP * n, KP * (n + 1))
                nc.vector.tensor_tensor(z[:], acc[m, n][:], bf1_b[:, cols], op=ALU.add)
                o = work.tile([P, KP], F32, name="o")
                nc.scalar.activation(o[:], z[:], ACT.Relu)
                nc.sync.dma_start(out=out[P * m : P * (m + 1), cols], in_=o[:])
